import numpy as np
import ml_dtypes


BF16 = ml_dtypes.bfloat16


def bf(x):
    return np.asarray(x, np.float32).astype(BF16)


def f64(x):
    return np.asarray(x).astype(np.float64)


E2M1 = np.array([0.0, 0.5, 1.0, 1.5, 2.0, 3.0, 4.0, 6.0, -0.0, -0.5, -1.0, -1.5, -2.0, -3.0, -4.0, -6.0])


def pack_weight(w, fmt):
    k, n = w.shape
    w = f64(bf(w)).reshape(k // 32, 32, n)
    amax = np.abs(w).max(1)
    if fmt == "e4m3":
        byte = np.frexp(amax)[1] - 1 + 127 - 7
    else:
        mant, ex = np.frexp(amax / 6.0)
        byte = np.where(mant > 0.5, ex, ex - 1) + 127
    byte = np.clip(np.where(amax > 0, byte, 1), 1, 254)
    scaled = (w * np.exp2(127.0 - byte)[:, None, :]).reshape(k, n).astype(np.float32)
    by_word = np.ascontiguousarray(scaled.reshape(k // 512, 128, 4, n).transpose(0, 1, 3, 2))
    if fmt == "e4m3":
        words = by_word.astype(ml_dtypes.float8_e4m3fn).view(np.uint8)
    else:
        c = by_word.astype(ml_dtypes.float4_e2m1fn).view(np.uint8) & 0xF
        words = c[..., 0::2] | (c[..., 1::2] << 4)
    return np.ascontiguousarray(words), np.ascontiguousarray(byte.astype(np.uint8).reshape(k // 512, 16, n))


def unpack_weight(words, scales, fmt):
    g, p, n, _ = words.shape
    if fmt == "e4m3":
        vals = np.ascontiguousarray(words).view(ml_dtypes.float8_e4m3fn).astype(np.float64)
    else:
        nib = np.empty((g, p, n, 4), np.uint8)
        nib[..., 0::2] = words & 0xF
        nib[..., 1::2] = words >> 4
        vals = E2M1[nib]
    vals = vals * np.repeat(np.exp2(scales.astype(np.float64) - 127.0), 8, axis=1)[..., None]
    return vals.transpose(0, 1, 3, 2).reshape(g * 512, n)

def pack4(w):
    words, scales = pack_weight(w, "e2m1")
    return words.reshape(words.shape[0], 128, -1), scales


def unpack4(words, scales):
    return unpack_weight(words.reshape(words.shape[0], 128, -1, 2), scales, "e2m1")


def kspread(k):
    return np.exp2(np.repeat(np.random.randint(-6, 7, k // 32), 32).astype(np.float64))


L, B, D, H, DK = 512, 2, 8192, 16, 64
DR = DK // 2
ROPE_BASE = 10000.0


def rope(t):
    theta = 1.0 / ROPE_BASE ** (np.arange(0, DR, 2) / DR)
    ang = np.arange(L)[:, None] * theta[None, :]
    ang2 = np.concatenate([ang, ang], axis=-1)
    cos = np.cos(ang2)[:, None, None, :]
    sin = np.sin(ang2)[:, None, None, :]
    t_rope, t_pass = t[..., :DR], t[..., DR:]
    neg_half = np.concatenate([-t_rope[..., DR // 2:], t_rope[..., :DR // 2]], axis=-1)
    return np.concatenate([t_rope * cos + neg_half * sin, t_pass], axis=-1)


def setup_inputs():
    s = kspread(D)
    x = np.random.standard_normal((L, B, D)) * s
    x_words, x_scales = pack4(np.ascontiguousarray(x.reshape(L * B, D).T))
    w = np.random.standard_normal((3 * H * DK, D)) / np.sqrt(D) / s[None, :]
    words, scales = pack4(np.ascontiguousarray(w.T))
    return {"x_words": x_words,
            "x_scales": x_scales,
            "in_proj_weight_words": words,
            "in_proj_weight_scales": scales}


def reference(x_words, x_scales, in_proj_weight_words, in_proj_weight_scales):
    qkv = unpack4(x_words, x_scales).T.reshape(L, B, D) @ unpack4(in_proj_weight_words, in_proj_weight_scales)
    qkv = qkv.reshape(L, B, H, 3 * DK)
    q, k, v = qkv[..., :DK], qkv[..., DK:2 * DK], qkv[..., 2 * DK:]
    q = rope(q)
    k = rope(k)
    return np.swapaxes(q, 0, 2), np.swapaxes(k, 0, 2), np.swapaxes(v, 0, 2)

@@ -1,0 +1,250 @@
+from contextlib import ExitStack
+import math
+
+import concourse.mybir as mybir
+
+F32 = mybir.dt.float32
+I32 = mybir.dt.int32
+U8 = mybir.dt.uint8
+FP4X4 = mybir.dt.float4_e2m1fn_x4
+ALU = mybir.AluOpType
+ACT = mybir.ActivationFunctionType
+
+P = 128
+PASSES = 16
+M_TILES = 8
+N_TILE = 512
+SEG = 64
+HEAD = 192
+ROPE_BASE = 10000.0
+
+FLOPS = 2 * 1024 * 3072 * 8192
+
+RUNS = ((0, 2), (2, 5), (5, 10), (10, 16))
+G_SPLIT = 10
+
+
+def tile_rotarypemultiheadselfattention_pa_kernel(
+    tc, x_words, x_scales, w_words, w_scales, out_q, out_k, out_v
+):
+    nc = tc.nc
+    outs = (out_q, out_k, out_v)
+
+    with ExitStack() as ctx:
+        ctx.enter_context(tc.manual_schedule())
+        keep = ctx.enter_context(tc.tile_pool(name="keep", bufs=1))
+        psum = ctx.enter_context(tc.psum_pool(name="psum", bufs=8))
+
+        def load_planes(dst, src, g0, g1, c0, c1):
+            for r in range(4):
+                nc.sync.dma_start(
+                    out=dst[r:P:32].bitcast(I32),
+                    in_=src[g0:g1, r:16:4, c0:c1].rearrange("g q n -> q g n").bitcast(I32),
+                )
+
+        x_codes = []
+        w0_codes = []
+        for g in range(PASSES):
+            xc = keep.tile([P, 2048], U8, name="xc%d" % g, align_bytes=64)
+            x_codes.append(xc)
+            wc = keep.tile([P, 1024], U8, name="w0c%d" % g, align_bytes=64)
+            w0_codes.append(wc)
+        run_planes = []
+        run_of = {}
+        for i, (g0, g1) in enumerate(RUNS):
+            pl = keep.tile([P, g1 - g0, 1536], U8, name="runpl%d" % i, align_bytes=64)
+            run_planes.append(pl)
+            for g in range(g0, g1):
+                run_of[g] = (i, g - g0)
+        w12_codes = {}
+        w12_planes = {}
+        for n in (1, 2):
+            for i in range(4):
+                t = keep.tile([P, 4, 1024], U8, name="w%dc%d" % (n, i), align_bytes=64)
+                w12_codes[(n, i)] = t
+            for i in range(2):
+                t = keep.tile([P, 8, 512], U8, name="w%dp%d" % (n, i), align_bytes=64)
+                w12_planes[(n, i)] = t
+        w345_codes = []
+        w345_planes = []
+        for i in range(8):
+            t = keep.tile([P, 2, 3072], U8, name="w345c%d" % i, align_bytes=64)
+            w345_codes.append(t)
+            t = keep.tile([P, 2, 1536], U8, name="w345p%d" % i, align_bytes=64)
+            w345_planes.append(t)
+        table = keep.tile([P, M_TILES, 64], F32, name="table")
+
+        for pl in run_planes:
+            nc.vector.memset(pl[:].bitcast(I32), 0)
+
+        def load_codes_a(g):
+            nc.sync.dma_start(out=x_codes[g][:].bitcast(I32), in_=x_words[g].bitcast(I32))
+            nc.sync.dma_start(out=w0_codes[g][:].bitcast(I32), in_=w_words[g, :, 0:1024].bitcast(I32))
+
+        def load_planes_a(i):
+            g0, g1 = RUNS[i]
+            load_planes(run_planes[i][:, :, 0:1024], x_scales, g0, g1, 0, 1024)
+            load_planes(run_planes[i][:, :, 1024:1536], w_scales, g0, g1, 0, 512)
+
+        load_codes_a(0)
+        load_planes_a(0)
+        load_codes_a(1)
+        for i in range(1, len(RUNS)):
+            load_planes_a(i)
+            for g in range(RUNS[i][0], RUNS[i][1]):
+                load_codes_a(g)
+
+        with tc.tile_pool(name="build", bufs=1) as build:
+            pos_i = build.tile([P, M_TILES], I32, name="pos_i")
+            nc.gpsimd.iota(pos_i[:], pattern=[[P, M_TILES]], base=0, channel_multiplier=1)
+            l_i = build.tile([P, M_TILES], I32, name="l_i")
+            nc.vector.tensor_single_scalar(out=l_i[:], in_=pos_i[:], scalar=1, op=ALU.arith_shift_right)
+            l_f = build.tile([P, M_TILES], F32, name="l_f")
+            nc.vector.tensor_copy(out=l_f[:], in_=l_i[:])
+            turns = build.tile([P, M_TILES, 16], F32, name="turns")
+            for j in range(16):
+                nc.vector.tensor_scalar(
+                    out=turns[:, :, j], in0=l_f[:],
+                    scalar1=ROPE_BASE ** (-j / 16.0) / (2.0 * math.pi), scalar2=None, op0=ALU.mult,
+                )
+            t4 = build.tile([P, M_TILES, 4, 16], F32, name="t4")
+            for q, off in enumerate((0.0, 0.25, 0.25, 0.0)):
+                nc.vector.tensor_scalar(out=t4[:, :, q, :], in0=turns[:], scalar1=off, scalar2=None, op0=ALU.add)
+            whole_i = build.tile([P, M_TILES * 64], I32, name="whole_i")
+            whole_f = build.tile([P, M_TILES * 64], F32, name="whole_f")
+            t4f = t4[:].rearrange("p m q j -> p (m q j)")
+            nc.vector.tensor_copy(out=whole_i[:], in_=t4f)
+            nc.vector.tensor_copy(out=whole_f[:], in_=whole_i[:])
+            nc.vector.tensor_tensor(out=t4f, in0=t4f, in1=whole_f[:], op=ALU.subtract)
+            nc.vector.scalar_tensor_tensor(
+                out=whole_f[:], in0=t4f, scalar=0.5, in1=t4f, op0=ALU.is_gt, op1=ALU.subtract
+            )
+            neg = whole_f[:].rearrange("p (m c) -> p m c", c=64)
+            nc.scalar.activation(out=table[:, :, 0:16], in_=neg[:, :, 0:16], func=ACT.Sin, scale=2.0 * math.pi)
+            nc.scalar.activation(out=table[:, :, 16:64], in_=neg[:, :, 16:64], func=ACT.Sin, scale=-2.0 * math.pi)
+
+        for n in (1, 2):
+            for i in range(2):
+                nc.vector.memset(w12_planes[(n, i)][:].bitcast(I32), 0)
+        for pl in w345_planes:
+            nc.vector.memset(pl[:].bitcast(I32), 0)
+
+        for n in (1, 2):
+            for i in range(2):
+                load_planes(w12_planes[(n, i)][:], w_scales, 8 * i, 8 * i + 8, 512 * n, 512 * n + 512)
+                for k in (2 * i, 2 * i + 1):
+                    nc.sync.dma_start(
+                        out=w12_codes[(n, k)][:].bitcast(I32),
+                        in_=w_words[4 * k:4 * k + 4, :, 1024 * n:1024 * n + 1024].rearrange("g p n -> p g n").bitcast(I32),
+                    )
+
+        def load_345(i):
+            load_planes(w345_planes[i][:], w_scales, 2 * i, 2 * i + 2, 1536, 3072)
+            nc.sync.dma_start(
+                out=w345_codes[i][:].bitcast(I32),
+                in_=w_words[2 * i:2 * i + 2, :, 3072:6144].rearrange("g p n -> p g n").bitcast(I32),
+            )
+
+        stage = ctx.enter_context(tc.tile_pool(name="stage", bufs=4))
+        tmp = ctx.enter_context(tc.tile_pool(name="tmp", bufs=2))
+
+        def mm(acc, m, g, n):
+            i, gl = run_of[g]
+            if n == 0:
+                rhs = w0_codes[g][:]
+                rhs_scale = run_planes[i][:, gl, 1024:1536]
+            elif n <= 2:
+                rhs = w12_codes[(n, g // 4)][:, g % 4, :]
+                rhs_scale = w12_planes[(n, g // 8)][:, g % 8, :]
+            else:
+                rhs = w345_codes[g // 2][:, g % 2, 1024 * (n - 3):1024 * (n - 2)]
+                rhs_scale = w345_planes[g // 2][:, g % 2, 512 * (n - 3):512 * (n - 2)]
+            nc.tensor.matmul_mx(
+                out=acc[:],
+                lhsT=x_codes[g][:, 256 * m:256 * (m + 1)].bitcast(FP4X4),
+                lhsT_scale=run_planes[i][:, gl, 128 * m:128 * (m + 1)],
+                rhs=rhs.bitcast(FP4X4),
+                rhs_scale=rhs_scale,
+                start=(g == 0),
+                stop=(g == PASSES - 1),
+            )
+
+        def kinds(c0, width):
+            s0 = c0 // SEG
+            s1 = (c0 + width) // SEG
+            found = []
+            for t in range(3):
+                first = s0 + ((t - s0) % 3)
+                found.append((first, len(range(first, s1, 3))))
+            return s0, found
+
+        def new_stage(width):
+            st = stage.tile([P, width + 2 * SEG], F32, name="st", tag="st")
+            return st
+
+        def rope(st, m, c0, width):
+            s0, found = kinds(c0, width)
+            (fq, nq), (fk, nk) = found[0], found[1]
+            assert fk == fq + 1 and nq == nk
+            off = (fq - s0) * SEG
+            qk = st[:, off:off + nq * HEAD].rearrange("p (h c) -> p h c", c=HEAD)[:, :, 0:2 * SEG]
+            qk = qk.rearrange("p h (t d) -> p h t d", t=2)
+            s32 = [P, nq, 2, 32]
+            s16 = [P, nq, 2, 16]
+            nsin = table[:, m, 0:16].unsqueeze(1).unsqueeze(1).to_broadcast(s16)
+            cos2 = table[:, m, 16:48].unsqueeze(1).unsqueeze(1).to_broadcast(s32)
+            sin = table[:, m, 48:64].unsqueeze(1).unsqueeze(1).to_broadcast(s16)
+            t1 = tmp.tile(s32, F32, name="t1", tag="t1")
+            t2 = tmp.tile(s32, F32, name="t2", tag="t2")
+            nc.vector.tensor_tensor(out=t1[:], in0=qk[:, :, :, 0:32], in1=cos2, op=ALU.mult)
+            nc.vector.tensor_tensor(out=t2[:, :, :, 0:16], in0=qk[:, :, :, 16:32], in1=nsin, op=ALU.mult)
+            nc.vector.tensor_tensor(out=t2[:, :, :, 16:32], in0=qk[:, :, :, 0:16], in1=sin, op=ALU.mult)
+            nc.vector.tensor_tensor(out=qk[:, :, :, 0:32], in0=t1[:], in1=t2[:], op=ALU.add)
+
+        def store(st, m, c0, width):
+            s0, found = kinds(c0, width)
+            for t in range(3):
+                first, count = found[t]
+                off = (first - s0) * SEG
+                h0 = first // 3
+                src = st[:, off:off + count * HEAD].rearrange("p (h c) -> p h c", c=HEAD)[:, :, 0:SEG]
+                for b in range(2):
+                    nc.sync.dma_start(
+                        out=outs[t][h0:h0 + count, b, 64 * m:64 * m + 64, :].rearrange("h l d -> l h d"),
+                        in_=src[b:P:2],
+                    )
+
+        def unit(m, blocks):
+            c0 = blocks[0] * N_TILE
+            width = len(blocks) * N_TILE
+            st = new_stage(width)
+            for k, n in enumerate(blocks):
+                acc = psum.tile([P, N_TILE], F32, name="acc", tag="acc")
+                for g in range(PASSES):
+                    mm(acc, m, g, n)
+                nc.scalar.copy(out=st[:, k * N_TILE:(k + 1) * N_TILE], in_=acc[:])
+            rope(st, m, c0, width)
+            store(st, m, c0, width)
+
+        accs = []
+        for m in range(M_TILES):
+            acc = psum.tile([P, N_TILE], F32, name="acc", tag="acc")
+            accs.append(acc)
+        for g in range(G_SPLIT):
+            for m in range(M_TILES):
+                mm(accs[m], m, g, 0)
+        for m in range(M_TILES):
+            for g in range(G_SPLIT, PASSES):
+                mm(accs[m], m, g, 0)
+            st = new_stage(N_TILE)
+            nc.scalar.copy(out=st[:, 0:N_TILE], in_=accs[m][:])
+            rope(st, m, 0, N_TILE)
+            store(st, m, 0, N_TILE)
+            load_345(m)
+
+        for m in range(M_TILES):
+            unit(m, (1, 2))
+        for m in range(M_TILES - 1):
+            unit(m, (3, 4, 5))
+        unit(M_TILES - 1, (4, 5))
+        unit(M_TILES - 1, (3,))

@@ -5,6 +5,7 @@ import concourse.mybir as mybir
 
 F32 = mybir.dt.float32
 I32 = mybir.dt.int32
+BF16 = mybir.dt.bfloat16
 U8 = mybir.dt.uint8
 FP4X4 = mybir.dt.float4_e2m1fn_x4
 ALU = mybir.AluOpType
@@ -22,6 +23,7 @@ FLOPS = 2 * 1024 * 3072 * 8192
 
 RUNS = ((0, 2), (2, 5), (5, 10), (10, 16))
 G_SPLIT = 10
+WARM = 9
 
 
 def tile_rotarypemultiheadselfattention_pa_kernel(
@@ -74,8 +76,14 @@ def tile_rotarypemultiheadselfattention_pa_kernel(
             w345_planes.append(t)
         table = keep.tile([P, M_TILES, 64], F32, name="table")
 
+        zeros = keep.tile([P, N_TILE], BF16, name="zeros")
+        nc.gpsimd.memset(zeros[:], 0.0)
         for pl in run_planes:
             nc.vector.memset(pl[:].bitcast(I32), 0)
+
+        warm = psum.tile([P, N_TILE], F32, name="acc", tag="acc")
+        for i in range(WARM):
+            nc.tensor.matmul(out=warm[:], lhsT=zeros[:, 0:P], rhs=zeros[:], start=True, stop=True)
 
         def load_codes_a(g):
             nc.sync.dma_start(out=x_codes[g][:].bitcast(I32), in_=x_words[g].bitcast(I32))
@@ -148,19 +156,22 @@ def tile_rotarypemultiheadselfattention_pa_kernel(
         stage = ctx.enter_context(tc.tile_pool(name="stage", bufs=4))
         tmp = ctx.enter_context(tc.tile_pool(name="tmp", bufs=2))
 
-        def mm(acc, m, g, n):
+        def mm(acc, m, g, c0, width):
             i, gl = run_of[g]
-            if n == 0:
-                rhs = w0_codes[g][:]
-                rhs_scale = run_planes[i][:, gl, 1024:1536]
-            elif n <= 2:
-                rhs = w12_codes[(n, g // 4)][:, g % 4, :]
-                rhs_scale = w12_planes[(n, g // 8)][:, g % 8, :]
+            if c0 < 512:
+                rhs = w0_codes[g][:, 2 * c0:2 * (c0 + width)]
+                rhs_scale = run_planes[i][:, gl, 1024 + c0:1024 + c0 + width]
+            elif c0 < 1536:
+                n = c0 // 512
+                c = c0 - 512 * n
+                rhs = w12_codes[(n, g // 4)][:, g % 4, 2 * c:2 * (c + width)]
+                rhs_scale = w12_planes[(n, g // 8)][:, g % 8, c:c + width]
             else:
-                rhs = w345_codes[g // 2][:, g % 2, 1024 * (n - 3):1024 * (n - 2)]
-                rhs_scale = w345_planes[g // 2][:, g % 2, 512 * (n - 3):512 * (n - 2)]
+                c = c0 - 1536
+                rhs = w345_codes[g // 2][:, g % 2, 2 * c:2 * (c + width)]
+                rhs_scale = w345_planes[g // 2][:, g % 2, c:c + width]
             nc.tensor.matmul_mx(
-                out=acc[:],
+                out=acc,
                 lhsT=x_codes[g][:, 256 * m:256 * (m + 1)].bitcast(FP4X4),
                 lhsT_scale=run_planes[i][:, gl, 128 * m:128 * (m + 1)],
                 rhs=rhs.bitcast(FP4X4),
@@ -182,49 +193,87 @@ def tile_rotarypemultiheadselfattention_pa_kernel(
             st = stage.tile([P, width + 2 * SEG], F32, name="st", tag="st")
             return st
 
-        def rope(st, m, c0, width):
-            s0, found = kinds(c0, width)
-            (fq, nq), (fk, nk) = found[0], found[1]
-            assert fk == fq + 1 and nq == nk
-            off = (fq - s0) * SEG
-            qk = st[:, off:off + nq * HEAD].rearrange("p (h c) -> p h c", c=HEAD)[:, :, 0:2 * SEG]
-            qk = qk.rearrange("p h (t d) -> p h t d", t=2)
-            s32 = [P, nq, 2, 32]
-            s16 = [P, nq, 2, 16]
+        def heads_view(ap, off, count, pair):
+            v = ap[:, off:off + count * HEAD].rearrange("p (h c) -> p h c", c=HEAD)[:, :, 0:pair * SEG]
+            return v.rearrange("p h (t d) -> p h t d", t=pair)
+
+        def rope_run(src, src_off, dst, dst_off, m, count, pair):
+            a = heads_view(src, src_off, count, pair)
+            o = heads_view(dst, dst_off, count, pair)
+            s32 = [P, count, pair, 32]
+            s16 = [P, count, pair, 16]
             nsin = table[:, m, 0:16].unsqueeze(1).unsqueeze(1).to_broadcast(s16)
             cos2 = table[:, m, 16:48].unsqueeze(1).unsqueeze(1).to_broadcast(s32)
             sin = table[:, m, 48:64].unsqueeze(1).unsqueeze(1).to_broadcast(s16)
             t1 = tmp.tile(s32, F32, name="t1", tag="t1")
             t2 = tmp.tile(s32, F32, name="t2", tag="t2")
-            nc.vector.tensor_tensor(out=t1[:], in0=qk[:, :, :, 0:32], in1=cos2, op=ALU.mult)
-            nc.vector.tensor_tensor(out=t2[:, :, :, 0:16], in0=qk[:, :, :, 16:32], in1=nsin, op=ALU.mult)
-            nc.vector.tensor_tensor(out=t2[:, :, :, 16:32], in0=qk[:, :, :, 0:16], in1=sin, op=ALU.mult)
-            nc.vector.tensor_tensor(out=qk[:, :, :, 0:32], in0=t1[:], in1=t2[:], op=ALU.add)
+            nc.vector.tensor_tensor(out=t2[:, :, :, 0:16], in0=a[:, :, :, 16:32], in1=nsin, op=ALU.mult)
+            nc.vector.tensor_tensor(out=t2[:, :, :, 16:32], in0=a[:, :, :, 0:16], in1=sin, op=ALU.mult)
+            nc.vector.tensor_tensor(out=t1[:], in0=a[:, :, :, 0:32], in1=cos2, op=ALU.mult)
+            nc.vector.tensor_tensor(out=o[:, :, :, 0:32], in0=t1[:], in1=t2[:], op=ALU.add)
 
-        def store(st, m, c0, width):
+        def rope(src, src_c0, dst, dst_c0, m, c0, width):
             s0, found = kinds(c0, width)
-            for t in range(3):
-                first, count = found[t]
-                off = (first - s0) * SEG
-                h0 = first // 3
-                src = st[:, off:off + count * HEAD].rearrange("p (h c) -> p h c", c=HEAD)[:, :, 0:SEG]
-                for b in range(2):
-                    nc.sync.dma_start(
-                        out=outs[t][h0:h0 + count, b, 64 * m:64 * m + 64, :].rearrange("h l d -> l h d"),
-                        in_=src[b:P:2],
-                    )
+            (fq, nq), (fk, nk) = found[0], found[1]
+            if fk == fq + 1 and nq == nk:
+                runs = ((fq, nq, 2),)
+            else:
+                runs = ((fq, nq, 1), (fk, nk, 1))
+            for (first, count, pair) in runs:
+                rope_run(src, first * SEG - src_c0, dst, first * SEG - dst_c0, m, count, pair)
 
-        def unit(m, blocks):
-            c0 = blocks[0] * N_TILE
-            width = len(blocks) * N_TILE
+        def store(st, m, c0, width, t, queue):
+            s0, found = kinds(c0, width)
+            first, count = found[t]
+            src = heads_view(st, (first - s0) * SEG, count, 1)[:, :, 0, :]
+            h0 = first // 3
+            for b in range(2):
+                queue.dma_start(
+                    out=outs[t][h0:h0 + count, b, 64 * m:64 * m + 64, :].rearrange("h l d -> l h d"),
+                    in_=src[b:P:2],
+                )
+
+        def group(m, c, w):
+            acc = psum.tile([P, N_TILE], F32, name="acc", tag="acc")
+            for g in range(PASSES):
+                mm(acc[:, 0:w], m, g, c, w)
+            return acc
+
+        def unit(m, pieces, each=False):
+            c0 = pieces[0][0]
+            width = sum([w for (c, w) in pieces])
             st = new_stage(width)
-            for k, n in enumerate(blocks):
-                acc = psum.tile([P, N_TILE], F32, name="acc", tag="acc")
-                for g in range(PASSES):
-                    mm(acc, m, g, n)
-                nc.scalar.copy(out=st[:, k * N_TILE:(k + 1) * N_TILE], in_=acc[:])
-            rope(st, m, c0, width)
-            store(st, m, c0, width)
+            for (c, w) in pieces:
+                acc = group(m, c, w)
+                nc.scalar.copy(out=st[:, c - c0:c - c0 + w], in_=acc[:, 0:w])
+                if each:
+                    rope(st, c0, st, c0, m, c, w)
+            if not each:
+                rope(st, c0, st, c0, m, c0, width)
+            for t in range(3):
+                store(st, m, c0, width, t, nc.sync)
+
+        def last_unit(m, c0):
+            st = new_stage(N_TILE)
+            acc = group(m, c0, 256)
+            nc.scalar.copy(out=st[:, 0:256], in_=acc[:, 0:256])
+            rope(st, c0, st, c0, m, c0, 256)
+            c1 = c0 + 256
+            acc = group(m, c1, 256)
+            rope(acc, c1, st, c0, m, c1, 256)
+            s1, found = kinds(c1, 256)
+            (fq, nq), (fk, nk), (fv, nv) = found
+            assert fk == fq + 1 and nq == nk
+            nc.scalar.copy(
+                out=heads_view(st, fv * SEG - c0, nv, 1), in_=heads_view(acc, fv * SEG - c1, nv, 1)
+            )
+            store(st, m, c0, N_TILE, 2, nc.scalar)
+            nc.scalar.copy(
+                out=heads_view(st, fq * SEG - c0, nq, 2)[:, :, :, 32:64],
+                in_=heads_view(acc, fq * SEG - c1, nq, 2)[:, :, :, 32:64],
+            )
+            store(st, m, c0, N_TILE, 0, nc.sync)
+            store(st, m, c0, N_TILE, 1, nc.scalar)
 
         accs = []
         for m in range(M_TILES):
@@ -232,19 +281,20 @@ def tile_rotarypemultiheadselfattention_pa_kernel(
             accs.append(acc)
         for g in range(G_SPLIT):
             for m in range(M_TILES):
-                mm(accs[m], m, g, 0)
+                mm(accs[m][:], m, g, 0, N_TILE)
         for m in range(M_TILES):
             for g in range(G_SPLIT, PASSES):
-                mm(accs[m], m, g, 0)
+                mm(accs[m][:], m, g, 0, N_TILE)
             st = new_stage(N_TILE)
             nc.scalar.copy(out=st[:, 0:N_TILE], in_=accs[m][:])
-            rope(st, m, 0, N_TILE)
-            store(st, m, 0, N_TILE)
+            rope(st, 0, st, 0, m, 0, N_TILE)
+            for t in range(3):
+                store(st, m, 0, N_TILE, t, nc.sync)
             load_345(m)
 
         for m in range(M_TILES):
-            unit(m, (1, 2))
+            unit(m, ((512, 512), (1024, 512)))
         for m in range(M_TILES - 1):
-            unit(m, (3, 4, 5))
-        unit(M_TILES - 1, (4, 5))
-        unit(M_TILES - 1, (3,))
+            unit(m, ((1536, 512), (2048, 512), (2560, 512)))
+        unit(M_TILES - 1, ((1536, 512), (2048, 512)), each=True)
+        last_unit(M_TILES - 1, 2560)

@@ -67,13 +67,17 @@ def tile_rotarypemultiheadselfattention_pa_kernel(
             for i in range(2):
                 t = keep.tile([P, 8, 512], U8, name="w%dp%d" % (n, i), align_bytes=64)
                 w12_planes[(n, i)] = t
-        w345_codes = []
-        w345_planes = []
-        for i in range(8):
-            t = keep.tile([P, 2, 3072], U8, name="w345c%d" % i, align_bytes=64)
-            w345_codes.append(t)
-            t = keep.tile([P, 2, 1536], U8, name="w345p%d" % i, align_bytes=64)
-            w345_planes.append(t)
+        kind_codes = []
+        kind_planes = []
+        for t in range(3):
+            kc = keep.tile([P, PASSES, 1024], U8, name="kindc%d" % t, align_bytes=64)
+            kind_codes.append(kc)
+            kp = keep.tile([P, PASSES, 512], U8, name="kindp%d" % t, align_bytes=64)
+            kind_planes.append(kp)
+        raw_planes = []
+        for i in range(2):
+            rp = keep.tile([P, 2, 1536], U8, name="rawp%d" % i, align_bytes=64)
+            raw_planes.append(rp)
         table = keep.tile([P, M_TILES, 64], F32, name="table")
 
         zeros = keep.tile([P, N_TILE], BF16, name="zeros")
@@ -134,7 +138,7 @@ def tile_rotarypemultiheadselfattention_pa_kernel(
         for n in (1, 2):
             for i in range(2):
                 nc.vector.memset(w12_planes[(n, i)][:].bitcast(I32), 0)
-        for pl in w345_planes:
+        for pl in raw_planes:
             nc.vector.memset(pl[:].bitcast(I32), 0)
 
         for n in (1, 2):
@@ -146,14 +150,28 @@ def tile_rotarypemultiheadselfattention_pa_kernel(
                         in_=w_words[4 * k:4 * k + 4, :, 1024 * n:1024 * n + 1024].rearrange("g p n -> p g n").bitcast(I32),
                     )
 
-        def load_345(i):
-            load_planes(w345_planes[i][:], w_scales, 2 * i, 2 * i + 2, 1536, 3072)
-            nc.sync.dma_start(
-                out=w345_codes[i][:].bitcast(I32),
-                in_=w_words[2 * i:2 * i + 2, :, 3072:6144].rearrange("g p n -> p g n").bitcast(I32),
-            )
+        def load_kind_codes(i):
+            for g in (2 * i, 2 * i + 1):
+                by_kind = w_words[g, :, 3072:6144].bitcast(I32).rearrange("p (h t c) -> p h t c", h=8, t=3)
+                for t in range(3):
+                    nc.sync.dma_start(
+                        out=kind_codes[t][:, g, :].bitcast(I32).rearrange("p (h c) -> p h c", h=8),
+                        in_=by_kind[:, :, t, :],
+                    )
+
+        def load_raw_planes(i):
+            load_planes(raw_planes[i % 2][:], w_scales, 2 * i, 2 * i + 2, 1536, 3072)
+
+        def sort_planes(i):
+            by_kind = raw_planes[i % 2][:].bitcast(I32).rearrange("p g (h t c) -> p g h t c", h=8, t=3)
+            for t in range(3):
+                nc.vector.tensor_copy(
+                    out=kind_planes[t][:, 2 * i:2 * i + 2, :].bitcast(I32).rearrange("p g (h c) -> p g h c", h=8),
+                    in_=by_kind[:, :, :, t, :],
+                )
 
         stage = ctx.enter_context(tc.tile_pool(name="stage", bufs=4))
+        sorted_stage = ctx.enter_context(tc.tile_pool(name="sorted_stage", bufs=4))
         tmp = ctx.enter_context(tc.tile_pool(name="tmp", bufs=2))
 
         def mm(acc, m, g, c0, width):
@@ -161,15 +179,15 @@ def tile_rotarypemultiheadselfattention_pa_kernel(
             if c0 < 512:
                 rhs = w0_codes[g][:, 2 * c0:2 * (c0 + width)]
                 rhs_scale = run_planes[i][:, gl, 1024 + c0:1024 + c0 + width]
-            elif c0 < 1536:
+            else:
                 n = c0 // 512
                 c = c0 - 512 * n
                 rhs = w12_codes[(n, g // 4)][:, g % 4, 2 * c:2 * (c + width)]
                 rhs_scale = w12_planes[(n, g // 8)][:, g % 8, c:c + width]
-            else:
-                c = c0 - 1536
-                rhs = w345_codes[g // 2][:, g % 2, 2 * c:2 * (c + width)]
-                rhs_scale = w345_planes[g // 2][:, g % 2, c:c + width]
+            mm_on(acc, m, g, rhs, rhs_scale)
+
+        def mm_on(acc, m, g, rhs, rhs_scale):
+            i, gl = run_of[g]
             nc.tensor.matmul_mx(
                 out=acc,
                 lhsT=x_codes[g][:, 256 * m:256 * (m + 1)].bitcast(FP4X4),
@@ -198,8 +216,9 @@ def tile_rotarypemultiheadselfattention_pa_kernel(
             return v.rearrange("p h (t d) -> p h t d", t=pair)
 
         def rope_run(src, src_off, dst, dst_off, m, count, pair):
-            a = heads_view(src, src_off, count, pair)
-            o = heads_view(dst, dst_off, count, pair)
+            rope_views(heads_view(src, src_off, count, pair), heads_view(dst, dst_off, count, pair), m, count, pair)
+
+        def rope_views(a, o, m, count, pair):
             s32 = [P, count, pair, 32]
             s16 = [P, count, pair, 16]
             nsin = table[:, m, 0:16].unsqueeze(1).unsqueeze(1).to_broadcast(s16)
@@ -253,27 +272,25 @@ def tile_rotarypemultiheadselfattention_pa_kernel(
             for t in range(3):
                 store(st, m, c0, width, t, nc.sync)
 
-        def last_unit(m, c0):
-            st = new_stage(N_TILE)
-            acc = group(m, c0, 256)
-            nc.scalar.copy(out=st[:, 0:256], in_=acc[:, 0:256])
-            rope(st, c0, st, c0, m, c0, 256)
-            c1 = c0 + 256
-            acc = group(m, c1, 256)
-            rope(acc, c1, st, c0, m, c1, 256)
-            s1, found = kinds(c1, 256)
-            (fq, nq), (fk, nk), (fv, nv) = found
-            assert fk == fq + 1 and nq == nk
-            nc.scalar.copy(
-                out=heads_view(st, fv * SEG - c0, nv, 1), in_=heads_view(acc, fv * SEG - c1, nv, 1)
-            )
-            store(st, m, c0, N_TILE, 2, nc.scalar)
-            nc.scalar.copy(
-                out=heads_view(st, fq * SEG - c0, nq, 2)[:, :, :, 32:64],
-                in_=heads_view(acc, fq * SEG - c1, nq, 2)[:, :, :, 32:64],
-            )
-            store(st, m, c0, N_TILE, 0, nc.sync)
-            store(st, m, c0, N_TILE, 1, nc.scalar)
+        def kind_unit(m, t, h0, heads, queues):
+            w = heads * SEG
+            acc = psum.tile([P, N_TILE], F32, name="acc", tag="acc")
+            for g in range(PASSES):
+                mm_on(
+                    acc[:, 0:w], m, g,
+                    kind_codes[t][:, g, 2 * SEG * h0:2 * SEG * (h0 + heads)],
+                    kind_planes[t][:, g, SEG * h0:SEG * (h0 + heads)],
+                )
+            so = sorted_stage.tile([P, 8, SEG], F32, name="so", tag="so")
+            nc.scalar.copy(out=so[:, 0:heads, :].rearrange("p h d -> p (h d)"), in_=acc[:, 0:w])
+            if t < 2:
+                v = so[:, 0:heads, :].rearrange("p (a h) d -> p a h d", a=1)
+                rope_views(v, v, m, 1, heads)
+            for b in range(2):
+                queues[b].dma_start(
+                    out=outs[t][8 + h0:8 + h0 + heads, b, 64 * m:64 * m + 64, :].rearrange("h l d -> l h d"),
+                    in_=so[b:P:2, 0:heads, :],
+                )
 
         accs = []
         for m in range(M_TILES):
@@ -290,11 +307,20 @@ def tile_rotarypemultiheadselfattention_pa_kernel(
             rope(st, 0, st, 0, m, 0, N_TILE)
             for t in range(3):
                 store(st, m, 0, N_TILE, t, nc.sync)
-            load_345(m)
+            load_kind_codes(m)
+            if m < 2:
+                load_raw_planes(m)
 
         for m in range(M_TILES):
+            sort_planes(m)
+            if m + 2 < 8:
+                load_raw_planes(m + 2)
             unit(m, ((512, 512), (1024, 512)))
+        both_sync = (nc.sync, nc.sync)
         for m in range(M_TILES - 1):
-            unit(m, ((1536, 512), (2048, 512), (2560, 512)))
-        unit(M_TILES - 1, ((1536, 512), (2048, 512)), each=True)
-        last_unit(M_TILES - 1, 2560)
+            for t in range(3):
+                kind_unit(m, t, 0, 8, both_sync)
+        kind_unit(M_TILES - 1, 0, 0, 8, both_sync)
+        kind_unit(M_TILES - 1, 1, 0, 8, both_sync)
+        kind_unit(M_TILES - 1, 2, 0, 4, both_sync)
+        kind_unit(M_TILES - 1, 2, 4, 4, (nc.scalar, nc.sync))

@@ -21,9 +21,10 @@ ROPE_BASE = 10000.0
 
 FLOPS = 2 * 1024 * 3072 * 8192
 
-RUNS = ((0, 2), (2, 5), (5, 10), (10, 16))
+X_RUNS = ((0, 2), (2, 5), (5, 10), (10, 16))
+W_RUNS = ((0, 1), (1, 5), (5, 10), (10, 16))
 G_SPLIT = 10
-WARM = 9
+WARM = 7
 
 
 def tile_rotarypemultiheadselfattention_pa_kernel(
@@ -51,13 +52,20 @@ def tile_rotarypemultiheadselfattention_pa_kernel(
             x_codes.append(xc)
             wc = keep.tile([P, 1024], U8, name="w0c%d" % g, align_bytes=64)
             w0_codes.append(wc)
-        run_planes = []
-        run_of = {}
-        for i, (g0, g1) in enumerate(RUNS):
-            pl = keep.tile([P, g1 - g0, 1536], U8, name="runpl%d" % i, align_bytes=64)
-            run_planes.append(pl)
+        run_x = []
+        run_w = []
+        x_plane = {}
+        w0_plane = {}
+        for i, (g0, g1) in enumerate(X_RUNS):
+            pl = keep.tile([P, g1 - g0, 1024], U8, name="runx%d" % i, align_bytes=64)
+            run_x.append(pl)
             for g in range(g0, g1):
-                run_of[g] = (i, g - g0)
+                x_plane[g] = pl[:, g - g0, :]
+        for i, (g0, g1) in enumerate(W_RUNS):
+            pl = keep.tile([P, g1 - g0, 512], U8, name="runw%d" % i, align_bytes=64)
+            run_w.append(pl)
+            for g in range(g0, g1):
+                w0_plane[g] = pl[:, g - g0, :]
         w12_codes = {}
         w12_planes = {}
         for n in (1, 2):
@@ -81,9 +89,11 @@ def tile_rotarypemultiheadselfattention_pa_kernel(
         table = keep.tile([P, M_TILES, 64], F32, name="table")
 
         zeros = keep.tile([P, N_TILE], BF16, name="zeros")
-        nc.gpsimd.memset(zeros[:], 0.0)
-        for pl in run_planes:
-            nc.vector.memset(pl[:].bitcast(I32), 0)
+        nc.vector.memset(run_x[0][:].bitcast(I32), 0)
+        nc.vector.memset(zeros[:].bitcast(I32), 0)
+        for i in range(1, len(X_RUNS)):
+            nc.vector.memset(run_w[i][:].bitcast(I32), 0)
+            nc.vector.memset(run_x[i][:].bitcast(I32), 0)
 
         warm = psum.tile([P, N_TILE], F32, name="acc", tag="acc")
         for i in range(WARM):
@@ -93,17 +103,26 @@ def tile_rotarypemultiheadselfattention_pa_kernel(
             nc.sync.dma_start(out=x_codes[g][:].bitcast(I32), in_=x_words[g].bitcast(I32))
             nc.sync.dma_start(out=w0_codes[g][:].bitcast(I32), in_=w_words[g, :, 0:1024].bitcast(I32))
 
-        def load_planes_a(i):
-            g0, g1 = RUNS[i]
-            load_planes(run_planes[i][:, :, 0:1024], x_scales, g0, g1, 0, 1024)
-            load_planes(run_planes[i][:, :, 1024:1536], w_scales, g0, g1, 0, 512)
+        w_rows = w_scales.rearrange("g q n -> (g q) n")
 
-        load_codes_a(0)
-        load_planes_a(0)
+        def load_w_window(q, queue, view):
+            queue.dma_start(
+                out=run_w[0][32 * q:32 * q + 32, 0, :].bitcast(view),
+                in_=w_rows[4 * q:4 * q + 32, 0:512].bitcast(view),
+            )
+
+        load_w_window(2, nc.gpsimd, F32)
+        load_w_window(3, nc.gpsimd, F32)
+        load_w_window(0, nc.sync, I32)
+        load_w_window(1, nc.sync, I32)
+        nc.sync.dma_start(out=w0_codes[0][:].bitcast(I32), in_=w_words[0, :, 0:1024].bitcast(I32))
+        nc.sync.dma_start(out=x_codes[0][:].bitcast(I32), in_=x_words[0].bitcast(I32))
+        load_planes(run_x[0][:], x_scales, X_RUNS[0][0], X_RUNS[0][1], 0, 1024)
         load_codes_a(1)
-        for i in range(1, len(RUNS)):
-            load_planes_a(i)
-            for g in range(RUNS[i][0], RUNS[i][1]):
+        for i in range(1, len(X_RUNS)):
+            load_planes(run_w[i][:], w_scales, W_RUNS[i][0], W_RUNS[i][1], 0, 512)
+            load_planes(run_x[i][:], x_scales, X_RUNS[i][0], X_RUNS[i][1], 0, 1024)
+            for g in range(X_RUNS[i][0], X_RUNS[i][1]):
                 load_codes_a(g)
 
         with tc.tile_pool(name="build", bufs=1) as build:
@@ -175,10 +194,9 @@ def tile_rotarypemultiheadselfattention_pa_kernel(
         tmp = ctx.enter_context(tc.tile_pool(name="tmp", bufs=2))
 
         def mm(acc, m, g, c0, width):
-            i, gl = run_of[g]
             if c0 < 512:
                 rhs = w0_codes[g][:, 2 * c0:2 * (c0 + width)]
-                rhs_scale = run_planes[i][:, gl, 1024 + c0:1024 + c0 + width]
+                rhs_scale = w0_plane[g][:, c0:c0 + width]
             else:
                 n = c0 // 512
                 c = c0 - 512 * n
@@ -187,11 +205,10 @@ def tile_rotarypemultiheadselfattention_pa_kernel(
             mm_on(acc, m, g, rhs, rhs_scale)
 
         def mm_on(acc, m, g, rhs, rhs_scale):
-            i, gl = run_of[g]
             nc.tensor.matmul_mx(
                 out=acc,
                 lhsT=x_codes[g][:, 256 * m:256 * (m + 1)].bitcast(FP4X4),
-                lhsT_scale=run_planes[i][:, gl, 128 * m:128 * (m + 1)],
+                lhsT_scale=x_plane[g][:, 128 * m:128 * (m + 1)],
                 rhs=rhs.bitcast(FP4X4),
                 rhs_scale=rhs_scale,
                 start=(g == 0),

@@ -89,8 +89,8 @@ def tile_rotarypemultiheadselfattention_pa_kernel(
         table = keep.tile([P, M_TILES, 64], F32, name="table")
 
         zeros = keep.tile([P, N_TILE], BF16, name="zeros")
+        nc.gpsimd.memset(zeros[:], 0.0)
         nc.vector.memset(run_x[0][:].bitcast(I32), 0)
-        nc.vector.memset(zeros[:].bitcast(I32), 0)
         for i in range(1, len(X_RUNS)):
             nc.vector.memset(run_w[i][:].bitcast(I32), 0)
             nc.vector.memset(run_x[i][:].bitcast(I32), 0)
@@ -111,12 +111,12 @@ def tile_rotarypemultiheadselfattention_pa_kernel(
                 in_=w_rows[4 * q:4 * q + 32, 0:512].bitcast(view),
             )
 
-        load_w_window(2, nc.gpsimd, F32)
-        load_w_window(3, nc.gpsimd, F32)
         load_w_window(0, nc.sync, I32)
         load_w_window(1, nc.sync, I32)
         nc.sync.dma_start(out=w0_codes[0][:].bitcast(I32), in_=w_words[0, :, 0:1024].bitcast(I32))
         nc.sync.dma_start(out=x_codes[0][:].bitcast(I32), in_=x_words[0].bitcast(I32))
+        load_w_window(2, nc.sync, I32)
+        load_w_window(3, nc.sync, I32)
         load_planes(run_x[0][:], x_scales, X_RUNS[0][0], X_RUNS[0][1], 0, 1024)
         load_codes_a(1)
         for i in range(1, len(X_RUNS)):

@@ -215,6 +215,15 @@ def tile_rotarypemultiheadselfattention_pa_kernel(
                 stop=(g == PASSES - 1),
             )
 
+        emptied = []
+
+        def empty_bank(out, in_):
+            if len(emptied) % 2 == 0:
+                nc.scalar.copy(out=out, in_=in_)
+            else:
+                nc.vector.tensor_copy(out=out, in_=in_)
+            emptied.append(1)
+
         def kinds(c0, width):
             s0 = c0 // SEG
             s1 = (c0 + width) // SEG
@@ -281,7 +290,7 @@ def tile_rotarypemultiheadselfattention_pa_kernel(
             st = new_stage(width)
             for (c, w) in pieces:
                 acc = group(m, c, w)
-                nc.scalar.copy(out=st[:, c - c0:c - c0 + w], in_=acc[:, 0:w])
+                empty_bank(st[:, c - c0:c - c0 + w], acc[:, 0:w])
                 if each:
                     rope(st, c0, st, c0, m, c, w)
             if not each:
@@ -299,7 +308,7 @@ def tile_rotarypemultiheadselfattention_pa_kernel(
                     kind_planes[t][:, g, SEG * h0:SEG * (h0 + heads)],
                 )
             so = sorted_stage.tile([P, 8, SEG], F32, name="so", tag="so")
-            nc.scalar.copy(out=so[:, 0:heads, :].rearrange("p h d -> p (h d)"), in_=acc[:, 0:w])
+            empty_bank(so[:, 0:heads, :].rearrange("p h d -> p (h d)"), acc[:, 0:w])
             if t < 2:
                 v = so[:, 0:heads, :].rearrange("p (a h) d -> p a h d", a=1)
                 rope_views(v, v, m, 1, heads)
@@ -320,7 +329,7 @@ def tile_rotarypemultiheadselfattention_pa_kernel(
             for g in range(G_SPLIT, PASSES):
                 mm(accs[m][:], m, g, 0, N_TILE)
             st = new_stage(N_TILE)
-            nc.scalar.copy(out=st[:, 0:N_TILE], in_=accs[m][:])
+            empty_bank(st[:, 0:N_TILE], accs[m][:])
             rope(st, 0, st, 0, m, 0, N_TILE)
             for t in range(3):
                 store(st, m, 0, N_TILE, t, nc.sync)

@@ -38,6 +38,13 @@ def tile_rotarypemultiheadselfattention_pa_kernel(
         keep = ctx.enter_context(tc.tile_pool(name="keep", bufs=1))
         psum = ctx.enter_context(tc.psum_pool(name="psum", bufs=8))
 
+        cursor = [0]
+
+        def placed(shape, dtype, width_bytes, name):
+            t = keep.tile(shape, dtype, name=name, align_bytes=256, offset=cursor[0])
+            cursor[0] += 256 * ((width_bytes + 255) // 256)
+            return t
+
         def load_planes(dst, src, g0, g1, c0, c1):
             for r in range(4):
                 nc.sync.dma_start(
@@ -48,21 +55,21 @@ def tile_rotarypemultiheadselfattention_pa_kernel(
         x_codes = []
         w0_codes = []
         for g in range(PASSES):
-            xc = keep.tile([P, 2048], U8, name="xc%d" % g, align_bytes=64)
+            xc = placed([P, 2048], U8, 2048, "xc%d" % g)
             x_codes.append(xc)
-            wc = keep.tile([P, 1024], U8, name="w0c%d" % g, align_bytes=64)
+            wc = placed([P, 1024], U8, 1024, "w0c%d" % g)
             w0_codes.append(wc)
         run_x = []
         run_w = []
         x_plane = {}
         w0_plane = {}
         for i, (g0, g1) in enumerate(X_RUNS):
-            pl = keep.tile([P, g1 - g0, 1024], U8, name="runx%d" % i, align_bytes=64)
+            pl = placed([P, g1 - g0, 1024], U8, (g1 - g0) * 1024, "runx%d" % i)
             run_x.append(pl)
             for g in range(g0, g1):
                 x_plane[g] = pl[:, g - g0, :]
         for i, (g0, g1) in enumerate(W_RUNS):
-            pl = keep.tile([P, g1 - g0, 512], U8, name="runw%d" % i, align_bytes=64)
+            pl = placed([P, g1 - g0, 512], U8, (g1 - g0) * 512, "runw%d" % i)
             run_w.append(pl)
             for g in range(g0, g1):
                 w0_plane[g] = pl[:, g - g0, :]
@@ -70,25 +77,25 @@ def tile_rotarypemultiheadselfattention_pa_kernel(
         w12_planes = {}
         for n in (1, 2):
             for i in range(4):
-                t = keep.tile([P, 4, 1024], U8, name="w%dc%d" % (n, i), align_bytes=64)
+                t = placed([P, 4, 1024], U8, 4096, "w%dc%d" % (n, i))
                 w12_codes[(n, i)] = t
             for i in range(2):
-                t = keep.tile([P, 8, 512], U8, name="w%dp%d" % (n, i), align_bytes=64)
+                t = placed([P, 8, 512], U8, 4096, "w%dp%d" % (n, i))
                 w12_planes[(n, i)] = t
         kind_codes = []
         kind_planes = []
         for t in range(3):
-            kc = keep.tile([P, PASSES, 1024], U8, name="kindc%d" % t, align_bytes=64)
+            kc = placed([P, PASSES, 1024], U8, PASSES * 1024, "kindc%d" % t)
             kind_codes.append(kc)
-            kp = keep.tile([P, PASSES, 512], U8, name="kindp%d" % t, align_bytes=64)
+            kp = placed([P, PASSES, 512], U8, PASSES * 512, "kindp%d" % t)
             kind_planes.append(kp)
         raw_planes = []
         for i in range(2):
-            rp = keep.tile([P, 2, 1536], U8, name="rawp%d" % i, align_bytes=64)
+            rp = placed([P, 2, 1536], U8, 3072, "rawp%d" % i)
             raw_planes.append(rp)
-        table = keep.tile([P, M_TILES, 64], F32, name="table")
+        table = placed([P, M_TILES, 64], F32, M_TILES * 256, "table")
 
-        zeros = keep.tile([P, N_TILE], BF16, name="zeros")
+        zeros = placed([P, N_TILE], BF16, 2 * N_TILE, "zeros")
         nc.gpsimd.memset(zeros[:], 0.0)
         nc.vector.memset(run_x[0][:].bitcast(I32), 0)
         for i in range(1, len(X_RUNS)):
@@ -234,7 +241,7 @@ def tile_rotarypemultiheadselfattention_pa_kernel(
             return s0, found
 
         def new_stage(width):
-            st = stage.tile([P, width + 2 * SEG], F32, name="st", tag="st")
+            st = stage.tile([P, width + 2 * SEG], F32, name="st", tag="st", align_bytes=256)
             return st
 
         def heads_view(ap, off, count, pair):
@@ -307,7 +314,7 @@ def tile_rotarypemultiheadselfattention_pa_kernel(
                     kind_codes[t][:, g, 2 * SEG * h0:2 * SEG * (h0 + heads)],
                     kind_planes[t][:, g, SEG * h0:SEG * (h0 + heads)],
                 )
-            so = sorted_stage.tile([P, 8, SEG], F32, name="so", tag="so")
+            so = sorted_stage.tile([P, 8, SEG], F32, name="so", tag="so", align_bytes=256)
             empty_bank(so[:, 0:heads, :].rearrange("p h d -> p (h d)"), acc[:, 0:w])
             if t < 2:
                 v = so[:, 0:heads, :].rearrange("p (a h) d -> p a h d", a=1)

@@ -356,4 +356,4 @@ def tile_rotarypemultiheadselfattention_pa_kernel(
         kind_unit(M_TILES - 1, 0, 0, 8, both_sync)
         kind_unit(M_TILES - 1, 1, 0, 8, both_sync)
         kind_unit(M_TILES - 1, 2, 0, 4, both_sync)
-        kind_unit(M_TILES - 1, 2, 4, 4, (nc.scalar, nc.sync))
+        kind_unit(M_TILES - 1, 2, 4, 4, (nc.scalar, nc.scalar))

@@ -122,9 +122,9 @@ def tile_rotarypemultiheadselfattention_pa_kernel(
         load_w_window(1, nc.sync, I32)
         nc.sync.dma_start(out=w0_codes[0][:].bitcast(I32), in_=w_words[0, :, 0:1024].bitcast(I32))
         nc.sync.dma_start(out=x_codes[0][:].bitcast(I32), in_=x_words[0].bitcast(I32))
-        load_w_window(2, nc.sync, I32)
-        load_w_window(3, nc.sync, I32)
         load_planes(run_x[0][:], x_scales, X_RUNS[0][0], X_RUNS[0][1], 0, 1024)
+        load_w_window(2, nc.scalar, F32)
+        load_w_window(3, nc.scalar, F32)
         load_codes_a(1)
         for i in range(1, len(X_RUNS)):
             load_planes(run_w[i][:], w_scales, W_RUNS[i][0], W_RUNS[i][1], 0, 512)

@@ -224,8 +224,8 @@ def tile_rotarypemultiheadselfattention_pa_kernel(
 
         emptied = []
 
-        def empty_bank(out, in_):
-            if len(emptied) % 2 == 0:
+        def empty_bank(out, in_, by_scalar=False):
+            if by_scalar or len(emptied) % 2 == 0:
                 nc.scalar.copy(out=out, in_=in_)
             else:
                 nc.vector.tensor_copy(out=out, in_=in_)
@@ -305,7 +305,7 @@ def tile_rotarypemultiheadselfattention_pa_kernel(
             for t in range(3):
                 store(st, m, c0, width, t, nc.sync)
 
-        def kind_unit(m, t, h0, heads, queues):
+        def kind_unit(m, t, h0, heads, queues, by_scalar=False):
             w = heads * SEG
             acc = psum.tile([P, N_TILE], F32, name="acc", tag="acc")
             for g in range(PASSES):
@@ -315,7 +315,7 @@ def tile_rotarypemultiheadselfattention_pa_kernel(
                     kind_planes[t][:, g, SEG * h0:SEG * (h0 + heads)],
                 )
             so = sorted_stage.tile([P, 8, SEG], F32, name="so", tag="so", align_bytes=256)
-            empty_bank(so[:, 0:heads, :].rearrange("p h d -> p (h d)"), acc[:, 0:w])
+            empty_bank(so[:, 0:heads, :].rearrange("p h d -> p (h d)"), acc[:, 0:w], by_scalar)
             if t < 2:
                 v = so[:, 0:heads, :].rearrange("p (a h) d -> p a h d", a=1)
                 rope_views(v, v, m, 1, heads)
@@ -356,4 +356,5 @@ def tile_rotarypemultiheadselfattention_pa_kernel(
         kind_unit(M_TILES - 1, 0, 0, 8, both_sync)
         kind_unit(M_TILES - 1, 1, 0, 8, both_sync)
         kind_unit(M_TILES - 1, 2, 0, 4, both_sync)
-        kind_unit(M_TILES - 1, 2, 4, 4, (nc.scalar, nc.scalar))
+        kind_unit(M_TILES - 1, 2, 4, 2, both_sync)
+        kind_unit(M_TILES - 1, 2, 6, 2, (nc.scalar, nc.scalar), True)

@@ -24,7 +24,7 @@ FLOPS = 2 * 1024 * 3072 * 8192
 X_RUNS = ((0, 2), (2, 5), (5, 10), (10, 16))
 W_RUNS = ((0, 1), (1, 5), (5, 10), (10, 16))
 G_SPLIT = 10
-WARM = 7
+WARM = 5
 
 
 def tile_rotarypemultiheadselfattention_pa_kernel(

from contextlib import ExitStack
import math

import concourse.mybir as mybir

F32 = mybir.dt.float32
I32 = mybir.dt.int32
BF16 = mybir.dt.bfloat16
U8 = mybir.dt.uint8
FP4X4 = mybir.dt.float4_e2m1fn_x4
ALU = mybir.AluOpType
ACT = mybir.ActivationFunctionType

P = 128
PASSES = 16
M_TILES = 8
N_TILE = 512
SEG = 64
HEAD = 192
ROPE_BASE = 10000.0

FLOPS = 2 * 1024 * 3072 * 8192

X_RUNS = ((0, 2), (2, 5), (5, 10), (10, 16))
W_RUNS = ((0, 1), (1, 5), (5, 10), (10, 16))
G_SPLIT = 10
WARM = 5


def tile_rotarypemultiheadselfattention_pa_kernel(
    tc, x_words, x_scales, w_words, w_scales, out_q, out_k, out_v
):
    nc = tc.nc
    outs = (out_q, out_k, out_v)

    with ExitStack() as ctx:
        ctx.enter_context(tc.manual_schedule())
        keep = ctx.enter_context(tc.tile_pool(name="keep", bufs=1))
        psum = ctx.enter_context(tc.psum_pool(name="psum", bufs=8))

        cursor = [0]

        def placed(shape, dtype, width_bytes, name):
            t = keep.tile(shape, dtype, name=name, align_bytes=256, offset=cursor[0])
            cursor[0] += 256 * ((width_bytes + 255) // 256)
            return t

        def load_planes(dst, src, g0, g1, c0, c1):
            for r in range(4):
                nc.sync.dma_start(
                    out=dst[r:P:32].bitcast(I32),
                    in_=src[g0:g1, r:16:4, c0:c1].rearrange("g q n -> q g n").bitcast(I32),
                )

        x_codes = []
        w0_codes = []
        for g in range(PASSES):
            xc = placed([P, 2048], U8, 2048, "xc%d" % g)
            x_codes.append(xc)
            wc = placed([P, 1024], U8, 1024, "w0c%d" % g)
            w0_codes.append(wc)
        run_x = []
        run_w = []
        x_plane = {}
        w0_plane = {}
        for i, (g0, g1) in enumerate(X_RUNS):
            pl = placed([P, g1 - g0, 1024], U8, (g1 - g0) * 1024, "runx%d" % i)
            run_x.append(pl)
            for g in range(g0, g1):
                x_plane[g] = pl[:, g - g0, :]
        for i, (g0, g1) in enumerate(W_RUNS):
            pl = placed([P, g1 - g0, 512], U8, (g1 - g0) * 512, "runw%d" % i)
            run_w.append(pl)
            for g in range(g0, g1):
                w0_plane[g] = pl[:, g - g0, :]
        w12_codes = {}
        w12_planes = {}
        for n in (1, 2):
            for i in range(4):
                t = placed([P, 4, 1024], U8, 4096, "w%dc%d" % (n, i))
                w12_codes[(n, i)] = t
            for i in range(2):
                t = placed([P, 8, 512], U8, 4096, "w%dp%d" % (n, i))
                w12_planes[(n, i)] = t
        kind_codes = []
        kind_planes = []
        for t in range(3):
            kc = placed([P, PASSES, 1024], U8, PASSES * 1024, "kindc%d" % t)
            kind_codes.append(kc)
            kp = placed([P, PASSES, 512], U8, PASSES * 512, "kindp%d" % t)
            kind_planes.append(kp)
        raw_planes = []
        for i in range(2):
            rp = placed([P, 2, 1536], U8, 3072, "rawp%d" % i)
            raw_planes.append(rp)
        table = placed([P, M_TILES, 64], F32, M_TILES * 256, "table")

        zeros = placed([P, N_TILE], BF16, 2 * N_TILE, "zeros")
        nc.gpsimd.memset(zeros[:], 0.0)
        nc.vector.memset(run_x[0][:].bitcast(I32), 0)
        for i in range(1, len(X_RUNS)):
            nc.vector.memset(run_w[i][:].bitcast(I32), 0)
            nc.vector.memset(run_x[i][:].bitcast(I32), 0)

        warm = psum.tile([P, N_TILE], F32, name="acc", tag="acc")
        for i in range(WARM):
            nc.tensor.matmul(out=warm[:], lhsT=zeros[:, 0:P], rhs=zeros[:], start=True, stop=True)

        def load_codes_a(g):
            nc.sync.dma_start(out=x_codes[g][:].bitcast(I32), in_=x_words[g].bitcast(I32))
            nc.sync.dma_start(out=w0_codes[g][:].bitcast(I32), in_=w_words[g, :, 0:1024].bitcast(I32))

        w_rows = w_scales.rearrange("g q n -> (g q) n")

        def load_w_window(q, queue, view):
            queue.dma_start(
                out=run_w[0][32 * q:32 * q + 32, 0, :].bitcast(view),
                in_=w_rows[4 * q:4 * q + 32, 0:512].bitcast(view),
            )

        load_w_window(0, nc.sync, I32)
        load_w_window(1, nc.sync, I32)
        nc.sync.dma_start(out=w0_codes[0][:].bitcast(I32), in_=w_words[0, :, 0:1024].bitcast(I32))
        nc.sync.dma_start(out=x_codes[0][:].bitcast(I32), in_=x_words[0].bitcast(I32))
        load_planes(run_x[0][:], x_scales, X_RUNS[0][0], X_RUNS[0][1], 0, 1024)
        load_w_window(2, nc.scalar, F32)
        load_w_window(3, nc.scalar, F32)
        load_codes_a(1)
        for i in range(1, len(X_RUNS)):
            load_planes(run_w[i][:], w_scales, W_RUNS[i][0], W_RUNS[i][1], 0, 512)
            load_planes(run_x[i][:], x_scales, X_RUNS[i][0], X_RUNS[i][1], 0, 1024)
            for g in range(X_RUNS[i][0], X_RUNS[i][1]):
                load_codes_a(g)

        with tc.tile_pool(name="build", bufs=1) as build:
            pos_i = build.tile([P, M_TILES], I32, name="pos_i")
            nc.gpsimd.iota(pos_i[:], pattern=[[P, M_TILES]], base=0, channel_multiplier=1)
            l_i = build.tile([P, M_TILES], I32, name="l_i")
            nc.vector.tensor_single_scalar(out=l_i[:], in_=pos_i[:], scalar=1, op=ALU.arith_shift_right)
            l_f = build.tile([P, M_TILES], F32, name="l_f")
            nc.vector.tensor_copy(out=l_f[:], in_=l_i[:])
            turns = build.tile([P, M_TILES, 16], F32, name="turns")
            for j in range(16):
                nc.vector.tensor_scalar(
                    out=turns[:, :, j], in0=l_f[:],
                    scalar1=ROPE_BASE ** (-j / 16.0) / (2.0 * math.pi), scalar2=None, op0=ALU.mult,
                )
            t4 = build.tile([P, M_TILES, 4, 16], F32, name="t4")
            for q, off in enumerate((0.0, 0.25, 0.25, 0.0)):
                nc.vector.tensor_scalar(out=t4[:, :, q, :], in0=turns[:], scalar1=off, scalar2=None, op0=ALU.add)
            whole_i = build.tile([P, M_TILES * 64], I32, name="whole_i")
            whole_f = build.tile([P, M_TILES * 64], F32, name="whole_f")
            t4f = t4[:].rearrange("p m q j -> p (m q j)")
            nc.vector.tensor_copy(out=whole_i[:], in_=t4f)
            nc.vector.tensor_copy(out=whole_f[:], in_=whole_i[:])
            nc.vector.tensor_tensor(out=t4f, in0=t4f, in1=whole_f[:], op=ALU.subtract)
            nc.vector.scalar_tensor_tensor(
                out=whole_f[:], in0=t4f, scalar=0.5, in1=t4f, op0=ALU.is_gt, op1=ALU.subtract
            )
            neg = whole_f[:].rearrange("p (m c) -> p m c", c=64)
            nc.scalar.activation(out=table[:, :, 0:16], in_=neg[:, :, 0:16], func=ACT.Sin, scale=2.0 * math.pi)
            nc.scalar.activation(out=table[:, :, 16:64], in_=neg[:, :, 16:64], func=ACT.Sin, scale=-2.0 * math.pi)

        for n in (1, 2):
            for i in range(2):
                nc.vector.memset(w12_planes[(n, i)][:].bitcast(I32), 0)
        for pl in raw_planes:
            nc.vector.memset(pl[:].bitcast(I32), 0)

        for n in (1, 2):
            for i in range(2):
                load_planes(w12_planes[(n, i)][:], w_scales, 8 * i, 8 * i + 8, 512 * n, 512 * n + 512)
                for k in (2 * i, 2 * i + 1):
                    nc.sync.dma_start(
                        out=w12_codes[(n, k)][:].bitcast(I32),
                        in_=w_words[4 * k:4 * k + 4, :, 1024 * n:1024 * n + 1024].rearrange("g p n -> p g n").bitcast(I32),
                    )

        def load_kind_codes(i):
            for g in (2 * i, 2 * i + 1):
                by_kind = w_words[g, :, 3072:6144].bitcast(I32).rearrange("p (h t c) -> p h t c", h=8, t=3)
                for t in range(3):
                    nc.sync.dma_start(
                        out=kind_codes[t][:, g, :].bitcast(I32).rearrange("p (h c) -> p h c", h=8),
                        in_=by_kind[:, :, t, :],
                    )

        def load_raw_planes(i):
            load_planes(raw_planes[i % 2][:], w_scales, 2 * i, 2 * i + 2, 1536, 3072)

        def sort_planes(i):
            by_kind = raw_planes[i % 2][:].bitcast(I32).rearrange("p g (h t c) -> p g h t c", h=8, t=3)
            for t in range(3):
                nc.vector.tensor_copy(
                    out=kind_planes[t][:, 2 * i:2 * i + 2, :].bitcast(I32).rearrange("p g (h c) -> p g h c", h=8),
                    in_=by_kind[:, :, :, t, :],
                )

        stage = ctx.enter_context(tc.tile_pool(name="stage", bufs=4))
        sorted_stage = ctx.enter_context(tc.tile_pool(name="sorted_stage", bufs=4))
        tmp = ctx.enter_context(tc.tile_pool(name="tmp", bufs=2))

        def mm(acc, m, g, c0, width):
            if c0 < 512:
                rhs = w0_codes[g][:, 2 * c0:2 * (c0 + width)]
                rhs_scale = w0_plane[g][:, c0:c0 + width]
            else:
                n = c0 // 512
                c = c0 - 512 * n
                rhs = w12_codes[(n, g // 4)][:, g % 4, 2 * c:2 * (c + width)]
                rhs_scale = w12_planes[(n, g // 8)][:, g % 8, c:c + width]
            mm_on(acc, m, g, rhs, rhs_scale)

        def mm_on(acc, m, g, rhs, rhs_scale):
            nc.tensor.matmul_mx(
                out=acc,
                lhsT=x_codes[g][:, 256 * m:256 * (m + 1)].bitcast(FP4X4),
                lhsT_scale=x_plane[g][:, 128 * m:128 * (m + 1)],
                rhs=rhs.bitcast(FP4X4),
                rhs_scale=rhs_scale,
                start=(g == 0),
                stop=(g == PASSES - 1),
            )

        emptied = []

        def empty_bank(out, in_, by_scalar=False):
            if by_scalar or len(emptied) % 2 == 0:
                nc.scalar.copy(out=out, in_=in_)
            else:
                nc.vector.tensor_copy(out=out, in_=in_)
            emptied.append(1)

        def kinds(c0, width):
            s0 = c0 // SEG
            s1 = (c0 + width) // SEG
            found = []
            for t in range(3):
                first = s0 + ((t - s0) % 3)
                found.append((first, len(range(first, s1, 3))))
            return s0, found

        def new_stage(width):
            st = stage.tile([P, width + 2 * SEG], F32, name="st", tag="st", align_bytes=256)
            return st

        def heads_view(ap, off, count, pair):
            v = ap[:, off:off + count * HEAD].rearrange("p (h c) -> p h c", c=HEAD)[:, :, 0:pair * SEG]
            return v.rearrange("p h (t d) -> p h t d", t=pair)

        def rope_run(src, src_off, dst, dst_off, m, count, pair):
            rope_views(heads_view(src, src_off, count, pair), heads_view(dst, dst_off, count, pair), m, count, pair)

        def rope_views(a, o, m, count, pair):
            s32 = [P, count, pair, 32]
            s16 = [P, count, pair, 16]
            nsin = table[:, m, 0:16].unsqueeze(1).unsqueeze(1).to_broadcast(s16)
            cos2 = table[:, m, 16:48].unsqueeze(1).unsqueeze(1).to_broadcast(s32)
            sin = table[:, m, 48:64].unsqueeze(1).unsqueeze(1).to_broadcast(s16)
            t1 = tmp.tile(s32, F32, name="t1", tag="t1")
            t2 = tmp.tile(s32, F32, name="t2", tag="t2")
            nc.vector.tensor_tensor(out=t2[:, :, :, 0:16], in0=a[:, :, :, 16:32], in1=nsin, op=ALU.mult)
            nc.vector.tensor_tensor(out=t2[:, :, :, 16:32], in0=a[:, :, :, 0:16], in1=sin, op=ALU.mult)
            nc.vector.tensor_tensor(out=t1[:], in0=a[:, :, :, 0:32], in1=cos2, op=ALU.mult)
            nc.vector.tensor_tensor(out=o[:, :, :, 0:32], in0=t1[:], in1=t2[:], op=ALU.add)

        def rope(src, src_c0, dst, dst_c0, m, c0, width):
            s0, found = kinds(c0, width)
            (fq, nq), (fk, nk) = found[0], found[1]
            if fk == fq + 1 and nq == nk:
                runs = ((fq, nq, 2),)
            else:
                runs = ((fq, nq, 1), (fk, nk, 1))
            for (first, count, pair) in runs:
                rope_run(src, first * SEG - src_c0, dst, first * SEG - dst_c0, m, count, pair)

        def store(st, m, c0, width, t, queue):
            s0, found = kinds(c0, width)
            first, count = found[t]
            src = heads_view(st, (first - s0) * SEG, count, 1)[:, :, 0, :]
            h0 = first // 3
            for b in range(2):
                queue.dma_start(
                    out=outs[t][h0:h0 + count, b, 64 * m:64 * m + 64, :].rearrange("h l d -> l h d"),
                    in_=src[b:P:2],
                )

        def group(m, c, w):
            acc = psum.tile([P, N_TILE], F32, name="acc", tag="acc")
            for g in range(PASSES):
                mm(acc[:, 0:w], m, g, c, w)
            return acc

        def unit(m, pieces, each=False):
            c0 = pieces[0][0]
            width = sum([w for (c, w) in pieces])
            st = new_stage(width)
            for (c, w) in pieces:
                acc = group(m, c, w)
                empty_bank(st[:, c - c0:c - c0 + w], acc[:, 0:w])
                if each:
                    rope(st, c0, st, c0, m, c, w)
            if not each:
                rope(st, c0, st, c0, m, c0, width)
            for t in range(3):
                store(st, m, c0, width, t, nc.sync)

        def kind_unit(m, t, h0, heads, queues, by_scalar=False):
            w = heads * SEG
            acc = psum.tile([P, N_TILE], F32, name="acc", tag="acc")
            for g in range(PASSES):
                mm_on(
                    acc[:, 0:w], m, g,
                    kind_codes[t][:, g, 2 * SEG * h0:2 * SEG * (h0 + heads)],
                    kind_planes[t][:, g, SEG * h0:SEG * (h0 + heads)],
                )
            so = sorted_stage.tile([P, 8, SEG], F32, name="so", tag="so", align_bytes=256)
            empty_bank(so[:, 0:heads, :].rearrange("p h d -> p (h d)"), acc[:, 0:w], by_scalar)
            if t < 2:
                v = so[:, 0:heads, :].rearrange("p (a h) d -> p a h d", a=1)
                rope_views(v, v, m, 1, heads)
            for b in range(2):
                queues[b].dma_start(
                    out=outs[t][8 + h0:8 + h0 + heads, b, 64 * m:64 * m + 64, :].rearrange("h l d -> l h d"),
                    in_=so[b:P:2, 0:heads, :],
                )

        accs = []
        for m in range(M_TILES):
            acc = psum.tile([P, N_TILE], F32, name="acc", tag="acc")
            accs.append(acc)
        for g in range(G_SPLIT):
            for m in range(M_TILES):
                mm(accs[m][:], m, g, 0, N_TILE)
        for m in range(M_TILES):
            for g in range(G_SPLIT, PASSES):
                mm(accs[m][:], m, g, 0, N_TILE)
            st = new_stage(N_TILE)
            empty_bank(st[:, 0:N_TILE], accs[m][:])
            rope(st, 0, st, 0, m, 0, N_TILE)
            for t in range(3):
                store(st, m, 0, N_TILE, t, nc.sync)
            load_kind_codes(m)
            if m < 2:
                load_raw_planes(m)

        for m in range(M_TILES):
            sort_planes(m)
            if m + 2 < 8:
                load_raw_planes(m + 2)
            unit(m, ((512, 512), (1024, 512)))
        both_sync = (nc.sync, nc.sync)
        for m in range(M_TILES - 1):
            for t in range(3):
                kind_unit(m, t, 0, 8, both_sync)
        kind_unit(M_TILES - 1, 0, 0, 8, both_sync)
        kind_unit(M_TILES - 1, 1, 0, 8, both_sync)
        kind_unit(M_TILES - 1, 2, 0, 4, both_sync)
        kind_unit(M_TILES - 1, 2, 4, 2, both_sync)
        kind_unit(M_TILES - 1, 2, 6, 2, (nc.scalar, nc.scalar), True)
